import numpy as np
import ml_dtypes


def mxq(x, axis, fmt="e4m3"):
    dtype, down = {"e4m3": (ml_dtypes.float8_e4m3fn, 7), "e5m2": (ml_dtypes.float8_e5m2, 14)}[fmt]
    v = np.moveaxis(np.asarray(x, np.float32).astype(ml_dtypes.bfloat16).astype(np.float64), axis, -1)
    blocks = v.reshape(v.shape[:-1] + (-1, 32))
    amax = np.abs(blocks).max(-1, keepdims=True)
    byte = np.maximum(np.where(amax > 0, np.frexp(amax)[1] - 1 + 127, 0) - down, 1)
    scale = np.exp2(byte - 127.0)
    codes = (blocks / scale).astype(np.float32).astype(dtype).astype(np.float64)
    return np.moveaxis((codes * scale).reshape(v.shape), -1, axis)


WIDE = False


def mx_kscale(k):
    if not WIDE:
        return np.ones(k)
    levels = np.array([10, -10, 5, -5, 0])
    if k % 512:
        return np.exp2(np.random.permutation(np.resize(levels, k // 32))).repeat(32)
    a = np.empty((k // 512, 16))
    for p in range(k // 512):
        a[p, :8] = np.random.permutation(np.resize(levels, 8))
        for g in range(8):
            far = levels[np.abs(levels - a[p, g]) >= 10]
            a[p, g + 8] = far[np.random.randint(len(far))]
    return np.exp2(a.ravel()).repeat(32)


BF16 = ml_dtypes.bfloat16


def bf(x):
    return np.asarray(x, np.float32).astype(BF16)


def f64(x):
    return np.asarray(x).astype(np.float64)


B, S, M, H, KV, HD = 2, 256, 2048, 16, 4, 128
E = H * HD


def sigmoid(v):
    return 1.0 / (1.0 + np.exp(-v))


def draw0():
    s, t = mx_kscale(M), mx_kscale(E)
    return {"hidden_states": bf(np.random.standard_normal((B, S, M)) * s),
            "Wq_gate": bf(np.random.standard_normal((M, H, HD)) / np.sqrt(M) / s[:, None, None]),
            "attn": bf(np.random.standard_normal((B, S, H, HD)) * 0.5 * t.reshape(H, HD)),
            "Wo": bf(np.random.standard_normal((H, HD, M)) * 2.0 / np.sqrt(E) / t.reshape(H, HD, 1))}


def core(hidden_states, Wq_gate, attn, Wo):
    gate = mxq(f64(hidden_states).reshape(B * S, M), 1, "e4m3") @ mxq(f64(Wq_gate).reshape(M, E), 0, "e4m3")
    g = f64(attn).reshape(B * S, E) * sigmoid(gate)
    return (mxq(g, 1, "e4m3") @ mxq(f64(Wo).reshape(E, M), 0, "e4m3")).reshape(B, S, M)


def e4m3fn_bytes(y):
    return np.clip(np.asarray(y, np.float64), -448.0, 448.0).astype(np.float32).astype(ml_dtypes.float8_e4m3fn).view(np.uint8)


def e4m3fn_values(b):
    return np.asarray(b, np.uint8).view(ml_dtypes.float8_e4m3fn).astype(np.float64)


def setup_inputs():
    d = draw0()
    x0 = np.asarray(d['Wq_gate']).astype(np.float64)
    s = (np.max(np.abs(x0), axis=(1, 2), keepdims=True) / 448.0).astype(np.float32)
    out = {}
    for k, v in d.items():
        if k == 'Wq_gate':
            out['Wq_gate_bytes'] = e4m3fn_bytes(x0 / s.astype(np.float64))
            out['Wq_gate_scale'] = s
        else:
            out[k] = v
    return out


def reference(hidden_states, Wq_gate_bytes, Wq_gate_scale, attn, Wo):
    return core(hidden_states, e4m3fn_values(Wq_gate_bytes) * Wq_gate_scale.astype(np.float64), attn, Wo)

@@ -1,0 +1,291 @@
+from contextlib import ExitStack
+
+import concourse.mybir as mybir
+from concourse.masks import make_identity
+
+F32 = mybir.dt.float32
+BF16 = mybir.dt.bfloat16
+U32 = mybir.dt.uint32
+U8 = mybir.dt.uint8
+FP8 = mybir.dt.float8_e4m3fn
+FP8X4 = mybir.dt.float8_e4m3fn_x4
+ACT = mybir.ActivationFunctionType
+MULT = mybir.AluOpType.mult
+
+P = 128
+T = 512
+D = 2048
+W = 512
+FLOPS = 2 * 2 * T * D * D
+
+UNITS = [(1, 0), (0, 0), (0, 1), (1, 1), (2, 1), (1, 2), (0, 2), (2, 2), (0, 3), (1, 3), (3, 0), (2, 0), (2, 3), (3, 2), (3, 1), (3, 3)]
+CHUNKS = [(0, 512), (512, 512), (1024, 512), (1536, 256), (1792, 256)]
+V_WIDEN = {(1, 2), (4, 3), (14, 1), (3, 1), (15, 1), (9, 2), (0, 2), (10, 0), (10, 3), (3, 2), (6, 2), (7, 1), (0, 0), (12, 0), (0, 3), (15, 3)}
+S_WO = {0, 1, 2, 4, 5, 9, 10, 14, 17, 19}
+V_FIN = {(4, 0), (4, 3), (3, 1), (4, 2), (3, 0)}
+X_STEPS = {4: [(0, 0), (0, 1), (0, 2), (0, 3)], 5: [(1, 0), (1, 1)], 6: [(1, 2), (1, 3)]}
+X_S = {(0, 1), (0, 2), (1, 2), (0, 0), (1, 0), (1, 1), (0, 3), (1, 3)}
+SIG_D = 1
+PROD_D = 2
+GQ_D = 3
+WO0 = 16
+S_LEAD = 1
+MX2_D = 4
+
+
+def tile_qwen3_5attention_pb_kernel(tc, hidden_states, Wq_gate_bytes, Wq_gate_scale, attn, Wo, out):
+    nc = tc.nc
+    wq_hbm = Wq_gate_bytes.rearrange("(s p j) u h -> s p j (u h)", p=P, j=4)
+    sc_hbm = Wq_gate_scale.rearrange("(s p j) a b -> p s (j a b)", p=P, j=4)
+    wo_hbm = Wo.rearrange("u h m -> (u h) m").rearrange("(s p j) m -> s p j m", p=P, j=4)
+    attn_hbm = attn.rearrange("b s u h -> b s (u h)")
+    out_hbm = out.rearrange("b s m -> (b s) m")
+
+    with ExitStack() as ctx:
+        keep = ctx.enter_context(tc.tile_pool(name="keep", bufs=1))
+        raw = ctx.enter_context(tc.tile_pool(name="raw", bufs=8))
+        stage = ctx.enter_context(tc.tile_pool(name="stage", bufs=4))
+        psum = ctx.enter_context(tc.psum_pool(name="psum", bufs=1))
+
+        ident = keep.tile([P, P], F32, name="ident")
+        make_identity(nc, ident[:])
+
+        ctx.enter_context(tc.manual_schedule())
+
+        scale = keep.tile([P, 4, 4], F32, name="scale")
+        nc.scalar.dma_start(out=scale[:], in_=sc_hbm)
+        warm = keep.tile([P, 1], F32, name="warm")
+        nc.vector.memset(warm[:], 0.0)
+        nc.scalar.activation(warm[:], warm[:], ACT.Sigmoid)
+
+        wraw = {}
+
+        def load_wq(s):
+            if s == 0:
+                for c in range(2):
+                    for h in range(2):
+                        t = keep.tile([P, 2, D // 2], U8, name=f"wraw0{c}{h}")
+                        nc.sync.dma_start(out=t[:], in_=wq_hbm[0][:, 2 * h : 2 * h + 2, c * 1024 : (c + 1) * 1024])
+                        for q in range(4):
+                            wraw[0, 2 * h + q // 2, 2 * c + q % 2] = t[:, q // 2, (q % 2) * W : (q % 2 + 1) * W]
+            else:
+                for h in range(2):
+                    t = keep.tile([P, 2, D], U8, name=f"wraw{s}{h}")
+                    nc.sync.dma_start(out=t[:], in_=wq_hbm[s][:, 2 * h : 2 * h + 2, :])
+                    for q in range(8):
+                        wraw[s, 2 * h + q // 4, q % 4] = t[:, q // 4, (q % 4) * W : (q % 4 + 1) * W]
+
+        def load_tok(src, b):
+            t = raw.tile([P, 2, D], BF16, name="raw")
+            for q in range(2):
+                nc.sync.dma_start(out=t[:, q, :], in_=src[b][q * P : (q + 1) * P, :])
+            return t
+
+        load_wq(0)
+        load_wq(1)
+        xraw = [load_tok(hidden_states, b) for b in range(2)]
+        load_wq(2)
+        load_wq(3)
+        araw = [load_tok(attn_hbm, b) for b in range(2)]
+        woraw = {}
+        for h in range(2):
+            for s in range(4):
+                t = raw.tile([P, 4, 1024], BF16, name="raw")
+                nc.sync.dma_start(out=t[:], in_=wo_hbm[s][:, :, h * 1024 : (h + 1) * 1024])
+                woraw[h, s] = t
+
+        def transposed(src, s, b, name):
+            bank = psum.tile([P, 512], F32, name=name)
+            for u in range(2):
+                for q in range(2):
+                    words = src[b][:, q, :].bitcast(F32)
+                    nc.tensor.transpose(bank[:, u * 256 + q * P : u * 256 + (q + 1) * P], words[:, 256 * s + u : 256 * (s + 1) : 2], ident[:])
+            return bank
+
+        def quantize(grp, cname, bufs, width):
+            codes = stage.tile([P, W], U32, name=cname, bufs=bufs, align_bytes=64)
+            scales = stage.tile([P, W], U8, name=cname + "s", bufs=bufs, align_bytes=64)
+            nc.vector.quantize_mx(out=codes[:, :width].bitcast(FP8X4), scales=scales[:, :width], in_=grp[:, : 4 * width])
+            return codes, scales
+
+        def new_grp():
+            return stage.tile([P, 4 * W], BF16, name="grp", bufs=5, align_bytes=64)
+
+        wd = {}
+        grp = {}
+        wq = {}
+
+        def widen(n):
+            g, s = UNITS[n]
+            t = stage.tile([P, 4, W], BF16, name="wd", bufs=3, align_bytes=64)
+            for j in range(4):
+                src = wraw[s, j, g].bitcast(FP8)
+                if (n, j) in V_WIDEN:
+                    nc.vector.tensor_scalar(out=t[:, j, :], in0=src, scalar1=scale[:, s, j : j + 1], scalar2=None, op0=MULT)
+                else:
+                    nc.scalar.activation(t[:, j, :], src, ACT.Copy, scale=scale[:, s, j : j + 1])
+            wd[n] = t
+
+        def interleave_wq(n):
+            t = new_grp()
+            nc.vector.tensor_copy(out=t[:].rearrange("p (t m j) -> p m j t", t=4, j=4), in_=wd[n][:].rearrange("p j (m t) -> p m j t", t=4))
+            grp[n] = t
+
+        def interleave_wo(w):
+            c, s = divmod(w, 4)
+            c0, width = CHUNKS[c]
+            t = new_grp()
+            src = woraw[c0 // 1024, s][:, :, c0 % 1024 : c0 % 1024 + width]
+            o = t[:, : 4 * width].rearrange("p (c i t) -> p c t i", i=4, t=4)
+            i = src.rearrange("p t (c i) -> p c t i", i=4)
+            if w in S_WO:
+                nc.scalar.copy(o, i)
+            else:
+                nc.vector.tensor_copy(out=o, in_=i)
+            grp["o", w] = t
+
+        xq = {}
+
+        xcodes = [stage.tile([P, W], U32, name=f"xq{s}", bufs=1, align_bytes=64) for s in range(4)]
+        xscales = [stage.tile([P, W], U8, name=f"xqs{s}", bufs=1, align_bytes=64) for s in range(4)]
+        xgrp = {}
+
+        def x_bank(b, s):
+            xgrp[b, s] = stage.tile([P, 2 * W], BF16, name="xgrp", bufs=4, align_bytes=64)
+            bank = transposed(xraw, s, b, f"b{s}")
+            dst = xgrp[b, s][:].bitcast(F32).rearrange("p (r u) -> p r u", u=2)
+            src = bank[:].rearrange("p (u r) -> p r u", u=2)
+            if (b, s) in X_S:
+                nc.scalar.copy(dst, src)
+            else:
+                nc.vector.tensor_copy(out=dst, in_=src)
+
+        def x_quantize(b, s):
+            nc.vector.quantize_mx(
+                out=xcodes[s][:, b * 256 : (b + 1) * 256].bitcast(FP8X4), scales=xscales[s][:, b * 256 : (b + 1) * 256], in_=xgrp[b, s][:]
+            )
+            if b == 1:
+                xq[s] = xcodes[s], xscales[s]
+
+        abank = {}
+        gq = {}
+        sig = {}
+        acc1 = {}
+
+        def mx1(g, s):
+            if s == 0:
+                for b in range(2):
+                    abank[g, b] = transposed(araw, g, b, f"b{2 * (g % 2) + b}")
+                for t in range(4):
+                    acc1[g, t] = psum.tile([P, T], F32, name=f"a{t}")
+            codes, scales = wq[g, s]
+            for t in range(4):
+                nc.tensor.matmul_mx(
+                    out=acc1[g, t][:],
+                    lhsT=codes[:, t * P : (t + 1) * P].bitcast(FP8X4),
+                    lhsT_scale=scales[:, t * P : (t + 1) * P],
+                    rhs=xq[s][0][:].bitcast(FP8X4),
+                    rhs_scale=xq[s][1][:],
+                    start=(s == 0),
+                    stop=(s == 3),
+                )
+
+        def sigmoid(g):
+            t = stage.tile([P, 4, T], F32, name="sig", bufs=2)
+            for k in range(4):
+                nc.scalar.activation(t[:, k, :], acc1[g, k][:], ACT.Sigmoid)
+            sig[g] = t
+
+        def product(g):
+            t = new_grp()
+            for b in range(2):
+                nc.vector.tensor_tensor(
+                    out=t[:, b * 1024 : (b + 1) * 1024].rearrange("p (r u e) -> p r u e", u=2, e=2),
+                    in0=abank[g, b][:].bitcast(BF16).rearrange("p (u r e) -> p r u e", u=2, e=2),
+                    in1=sig[g][:, :, b * 256 : (b + 1) * 256].rearrange("p (u e) r -> p r u e", u=2),
+                    op=MULT,
+                )
+            grp["g", g] = t
+
+        acc2 = {}
+
+        def mx2(w):
+            c, s = divmod(w, 4)
+            width = CHUNKS[c][1]
+            for i in range(4):
+                if s == 0:
+                    acc2[c, i] = psum.tile([P, W], F32, name=f"{'ab'[c % 2]}{i}")
+                codes, scales = grp["wo", w]
+                nc.tensor.matmul_mx(
+                    out=acc2[c, i][:, :width],
+                    lhsT=gq[s][0][:, i * P : (i + 1) * P].bitcast(FP8X4),
+                    lhsT_scale=gq[s][1][:, i * P : (i + 1) * P],
+                    rhs=codes[:, :width].bitcast(FP8X4),
+                    rhs_scale=scales[:, :width],
+                    start=(s == 0),
+                    stop=(s == 3),
+                )
+
+        def finish(c):
+            c0, width = CHUNKS[c]
+            for i in range(4):
+                o = stage.tile([P, W], F32, name="ost", bufs=8)
+                if (c, i) in V_FIN:
+                    nc.vector.tensor_copy(out=o[:, :width], in_=acc2[c, i][:, :width])
+                else:
+                    nc.scalar.copy(o[:, :width], acc2[c, i][:, :width])
+                nc.sync.dma_start(out=out_hbm[i * P : (i + 1) * P, c0 : c0 + width], in_=o[:, :width])
+
+        n_wo = 4 * len(CHUNKS)
+        events = {}
+        pending = {g: [] for g in range(4)}
+        open_group = 0
+        flushed = {g: 0 for g in range(4)}
+
+        def at(n, f, *a):
+            events.setdefault(n, []).append((f, a))
+
+        def put_gq(g):
+            gq[g] = quantize(grp["g", g], f"gq{g}", 1, W)
+
+        next_mx2 = 0
+        ready_at = {}
+        n = 0
+        while n < 60:
+            if n < 16:
+                widen(n)
+            for b, s in X_STEPS.get(n, []):
+                x_bank(b, s)
+            if 0 <= n - 1 < 16:
+                interleave_wq(n - 1)
+            for w in range(n_wo):
+                if WO0 + w - (S_LEAD if w in S_WO else 0) == n:
+                    interleave_wo(w)
+            if 0 <= n - 2 < 16:
+                wq[UNITS[n - 2]] = quantize(grp[n - 2], "wqc", 10, W)
+                pending[UNITS[n - 2][0]].append(UNITS[n - 2][1])
+            for b, s in X_STEPS.get(n - 1, []):
+                x_quantize(b, s)
+            if open_group < 4:
+                while flushed[open_group] < len(pending[open_group]) and flushed[open_group] in xq:
+                    mx1(open_group, flushed[open_group])
+                    flushed[open_group] += 1
+                if flushed[open_group] == 4:
+                    at(n + SIG_D, sigmoid, open_group)
+                    at(n + PROD_D, product, open_group)
+                    at(n + GQ_D, put_gq, open_group)
+                    flushed[open_group] = 5
+            for f, a in events.get(n, []):
+                f(*a)
+                if f is sigmoid:
+                    open_group += 1
+            w = n - WO0 - 1
+            if 0 <= w < n_wo:
+                grp["wo", w] = quantize(grp["o", w], "woc", 8, CHUNKS[w // 4][1])
+                ready_at[w] = n + MX2_D - 1
+            while next_mx2 in ready_at and ready_at[next_mx2] <= n and (next_mx2 % 4) in gq:
+                mx2(next_mx2)
+                if next_mx2 % 4 == 3:
+                    finish(next_mx2 // 4)
+                next_mx2 += 1
+            n += 1

@@ -31,6 +31,12 @@ GQ_D = 3
 WO0 = 16
 S_LEAD = 1
 MX2_D = 4
+RAWB = 8
+WDB = 3
+GRPB = 5
+OSTB = 8
+LAG = 1
+QLAG = 2
 
 
 def tile_qwen3_5attention_pb_kernel(tc, hidden_states, Wq_gate_bytes, Wq_gate_scale, attn, Wo, out):
@@ -43,7 +49,7 @@ def tile_qwen3_5attention_pb_kernel(tc, hidden_states, Wq_gate_bytes, Wq_gate_sc
 
     with ExitStack() as ctx:
         keep = ctx.enter_context(tc.tile_pool(name="keep", bufs=1))
-        raw = ctx.enter_context(tc.tile_pool(name="raw", bufs=8))
+        raw = ctx.enter_context(tc.tile_pool(name="raw", bufs=RAWB))
         stage = ctx.enter_context(tc.tile_pool(name="stage", bufs=4))
         psum = ctx.enter_context(tc.psum_pool(name="psum", bufs=1))
 
@@ -94,12 +100,13 @@ def tile_qwen3_5attention_pb_kernel(tc, hidden_states, Wq_gate_bytes, Wq_gate_sc
                 nc.sync.dma_start(out=t[:], in_=wo_hbm[s][:, :, h * 1024 : (h + 1) * 1024])
                 woraw[h, s] = t
 
-        def transposed(src, s, b, name):
+        def transposed(src, s, b, name, pairs):
             bank = psum.tile([P, 512], F32, name=name)
             for u in range(2):
                 for q in range(2):
                     words = src[b][:, q, :].bitcast(F32)
-                    nc.tensor.transpose(bank[:, u * 256 + q * P : u * 256 + (q + 1) * P], words[:, 256 * s + u : 256 * (s + 1) : 2], ident[:])
+                    dst = bank[:].rearrange("p (r u) -> p u r", u=2)[:, u] if pairs else bank[:, u * 256 : (u + 1) * 256]
+                    nc.tensor.transpose(dst[:, q * P : (q + 1) * P], words[:, 256 * s + u : 256 * (s + 1) : 2], ident[:])
             return bank
 
         def quantize(grp, cname, bufs, width):
@@ -109,7 +116,7 @@ def tile_qwen3_5attention_pb_kernel(tc, hidden_states, Wq_gate_bytes, Wq_gate_sc
             return codes, scales
 
         def new_grp():
-            return stage.tile([P, 4 * W], BF16, name="grp", bufs=5, align_bytes=64)
+            return stage.tile([P, 4 * W], BF16, name="grp", bufs=GRPB, align_bytes=64)
 
         wd = {}
         grp = {}
@@ -117,7 +124,7 @@ def tile_qwen3_5attention_pb_kernel(tc, hidden_states, Wq_gate_bytes, Wq_gate_sc
 
         def widen(n):
             g, s = UNITS[n]
-            t = stage.tile([P, 4, W], BF16, name="wd", bufs=3, align_bytes=64)
+            t = stage.tile([P, 4, W], BF16, name="wd", bufs=WDB, align_bytes=64)
             for j in range(4):
                 src = wraw[s, j, g].bitcast(FP8)
                 if (n, j) in V_WIDEN:
@@ -152,7 +159,7 @@ def tile_qwen3_5attention_pb_kernel(tc, hidden_states, Wq_gate_bytes, Wq_gate_sc
 
         def x_bank(b, s):
             xgrp[b, s] = stage.tile([P, 2 * W], BF16, name="xgrp", bufs=4, align_bytes=64)
-            bank = transposed(xraw, s, b, f"b{s}")
+            bank = transposed(xraw, s, b, f"b{s}", False)
             dst = xgrp[b, s][:].bitcast(F32).rearrange("p (r u) -> p r u", u=2)
             src = bank[:].rearrange("p (u r) -> p r u", u=2)
             if (b, s) in X_S:
@@ -175,7 +182,7 @@ def tile_qwen3_5attention_pb_kernel(tc, hidden_states, Wq_gate_bytes, Wq_gate_sc
         def mx1(g, s):
             if s == 0:
                 for b in range(2):
-                    abank[g, b] = transposed(araw, g, b, f"b{2 * (g % 2) + b}")
+                    abank[g, b] = transposed(araw, g, b, f"b{2 * (g % 2) + b}", True)
                 for t in range(4):
                     acc1[g, t] = psum.tile([P, T], F32, name=f"a{t}")
             codes, scales = wq[g, s]
@@ -200,9 +207,9 @@ def tile_qwen3_5attention_pb_kernel(tc, hidden_states, Wq_gate_bytes, Wq_gate_sc
             t = new_grp()
             for b in range(2):
                 nc.vector.tensor_tensor(
-                    out=t[:, b * 1024 : (b + 1) * 1024].rearrange("p (r u e) -> p r u e", u=2, e=2),
-                    in0=abank[g, b][:].bitcast(BF16).rearrange("p (u r e) -> p r u e", u=2, e=2),
-                    in1=sig[g][:, :, b * 256 : (b + 1) * 256].rearrange("p (u e) r -> p r u e", u=2),
+                    out=t[:, b * 1024 : (b + 1) * 1024].rearrange("p (r i t) -> p r t i", i=4, t=4),
+                    in0=abank[g, b][:].bitcast(BF16).rearrange("p (r i t) -> p r t i", i=4, t=4),
+                    in1=sig[g][:, :, b * 256 : (b + 1) * 256].rearrange("p t (r i) -> p r t i", i=4),
                     op=MULT,
                 )
             grp["g", g] = t
@@ -229,7 +236,7 @@ def tile_qwen3_5attention_pb_kernel(tc, hidden_states, Wq_gate_bytes, Wq_gate_sc
         def finish(c):
             c0, width = CHUNKS[c]
             for i in range(4):
-                o = stage.tile([P, W], F32, name="ost", bufs=8)
+                o = stage.tile([P, W], F32, name="ost", bufs=OSTB)
                 if (c, i) in V_FIN:
                     nc.vector.tensor_copy(out=o[:, :width], in_=acc2[c, i][:, :width])
                 else:
@@ -256,14 +263,14 @@ def tile_qwen3_5attention_pb_kernel(tc, hidden_states, Wq_gate_bytes, Wq_gate_sc
                 widen(n)
             for b, s in X_STEPS.get(n, []):
                 x_bank(b, s)
-            if 0 <= n - 1 < 16:
-                interleave_wq(n - 1)
+            if 0 <= n - LAG < 16:
+                interleave_wq(n - LAG)
             for w in range(n_wo):
                 if WO0 + w - (S_LEAD if w in S_WO else 0) == n:
                     interleave_wo(w)
-            if 0 <= n - 2 < 16:
-                wq[UNITS[n - 2]] = quantize(grp[n - 2], "wqc", 10, W)
-                pending[UNITS[n - 2][0]].append(UNITS[n - 2][1])
+            if 0 <= n - QLAG < 16:
+                wq[UNITS[n - QLAG]] = quantize(grp[n - QLAG], "wqc", 10, W)
+                pending[UNITS[n - QLAG][0]].append(UNITS[n - QLAG][1])
             for b, s in X_STEPS.get(n - 1, []):
                 x_quantize(b, s)
             if open_group < 4:

from contextlib import ExitStack

import concourse.mybir as mybir
from concourse.masks import make_identity

F32 = mybir.dt.float32
BF16 = mybir.dt.bfloat16
U32 = mybir.dt.uint32
U8 = mybir.dt.uint8
FP8 = mybir.dt.float8_e4m3fn
FP8X4 = mybir.dt.float8_e4m3fn_x4
ACT = mybir.ActivationFunctionType
MULT = mybir.AluOpType.mult

P = 128
T = 512
D = 2048
W = 512
FLOPS = 2 * 2 * T * D * D

UNITS = [(1, 0), (0, 0), (0, 1), (1, 1), (2, 1), (1, 2), (0, 2), (2, 2), (0, 3), (1, 3), (3, 0), (2, 0), (2, 3), (3, 2), (3, 1), (3, 3)]
CHUNKS = [(0, 512), (512, 512), (1024, 512), (1536, 256), (1792, 256)]
V_WIDEN = {(1, 2), (4, 3), (14, 1), (3, 1), (15, 1), (9, 2), (0, 2), (10, 0), (10, 3), (3, 2), (6, 2), (7, 1), (0, 0), (12, 0), (0, 3), (15, 3)}
S_WO = {0, 1, 2, 4, 5, 9, 10, 14, 17, 19}
V_FIN = {(4, 0), (4, 3), (3, 1), (4, 2), (3, 0)}
X_STEPS = {4: [(0, 0), (0, 1), (0, 2), (0, 3)], 5: [(1, 0), (1, 1)], 6: [(1, 2), (1, 3)]}
X_S = {(0, 1), (0, 2), (1, 2), (0, 0), (1, 0), (1, 1), (0, 3), (1, 3)}
SIG_D = 1
PROD_D = 2
GQ_D = 3
WO0 = 16
S_LEAD = 1
MX2_D = 4
RAWB = 8
WDB = 3
GRPB = 5
OSTB = 8
LAG = 1
QLAG = 2


def tile_qwen3_5attention_pb_kernel(tc, hidden_states, Wq_gate_bytes, Wq_gate_scale, attn, Wo, out):
    nc = tc.nc
    wq_hbm = Wq_gate_bytes.rearrange("(s p j) u h -> s p j (u h)", p=P, j=4)
    sc_hbm = Wq_gate_scale.rearrange("(s p j) a b -> p s (j a b)", p=P, j=4)
    wo_hbm = Wo.rearrange("u h m -> (u h) m").rearrange("(s p j) m -> s p j m", p=P, j=4)
    attn_hbm = attn.rearrange("b s u h -> b s (u h)")
    out_hbm = out.rearrange("b s m -> (b s) m")

    with ExitStack() as ctx:
        keep = ctx.enter_context(tc.tile_pool(name="keep", bufs=1))
        raw = ctx.enter_context(tc.tile_pool(name="raw", bufs=RAWB))
        stage = ctx.enter_context(tc.tile_pool(name="stage", bufs=4))
        psum = ctx.enter_context(tc.psum_pool(name="psum", bufs=1))

        ident = keep.tile([P, P], F32, name="ident")
        make_identity(nc, ident[:])

        ctx.enter_context(tc.manual_schedule())

        scale = keep.tile([P, 4, 4], F32, name="scale")
        nc.scalar.dma_start(out=scale[:], in_=sc_hbm)
        warm = keep.tile([P, 1], F32, name="warm")
        nc.vector.memset(warm[:], 0.0)
        nc.scalar.activation(warm[:], warm[:], ACT.Sigmoid)

        wraw = {}

        def load_wq(s):
            if s == 0:
                for c in range(2):
                    for h in range(2):
                        t = keep.tile([P, 2, D // 2], U8, name=f"wraw0{c}{h}")
                        nc.sync.dma_start(out=t[:], in_=wq_hbm[0][:, 2 * h : 2 * h + 2, c * 1024 : (c + 1) * 1024])
                        for q in range(4):
                            wraw[0, 2 * h + q // 2, 2 * c + q % 2] = t[:, q // 2, (q % 2) * W : (q % 2 + 1) * W]
            else:
                for h in range(2):
                    t = keep.tile([P, 2, D], U8, name=f"wraw{s}{h}")
                    nc.sync.dma_start(out=t[:], in_=wq_hbm[s][:, 2 * h : 2 * h + 2, :])
                    for q in range(8):
                        wraw[s, 2 * h + q // 4, q % 4] = t[:, q // 4, (q % 4) * W : (q % 4 + 1) * W]

        def load_tok(src, b):
            t = raw.tile([P, 2, D], BF16, name="raw")
            for q in range(2):
                nc.sync.dma_start(out=t[:, q, :], in_=src[b][q * P : (q + 1) * P, :])
            return t

        load_wq(0)
        load_wq(1)
        xraw = [load_tok(hidden_states, b) for b in range(2)]
        load_wq(2)
        load_wq(3)
        araw = [load_tok(attn_hbm, b) for b in range(2)]
        woraw = {}
        for h in range(2):
            for s in range(4):
                t = raw.tile([P, 4, 1024], BF16, name="raw")
                nc.sync.dma_start(out=t[:], in_=wo_hbm[s][:, :, h * 1024 : (h + 1) * 1024])
                woraw[h, s] = t

        def transposed(src, s, b, name, pairs):
            bank = psum.tile([P, 512], F32, name=name)
            for u in range(2):
                for q in range(2):
                    words = src[b][:, q, :].bitcast(F32)
                    dst = bank[:].rearrange("p (r u) -> p u r", u=2)[:, u] if pairs else bank[:, u * 256 : (u + 1) * 256]
                    nc.tensor.transpose(dst[:, q * P : (q + 1) * P], words[:, 256 * s + u : 256 * (s + 1) : 2], ident[:])
            return bank

        def quantize(grp, cname, bufs, width):
            codes = stage.tile([P, W], U32, name=cname, bufs=bufs, align_bytes=64)
            scales = stage.tile([P, W], U8, name=cname + "s", bufs=bufs, align_bytes=64)
            nc.vector.quantize_mx(out=codes[:, :width].bitcast(FP8X4), scales=scales[:, :width], in_=grp[:, : 4 * width])
            return codes, scales

        def new_grp():
            return stage.tile([P, 4 * W], BF16, name="grp", bufs=GRPB, align_bytes=64)

        wd = {}
        grp = {}
        wq = {}

        def widen(n):
            g, s = UNITS[n]
            t = stage.tile([P, 4, W], BF16, name="wd", bufs=WDB, align_bytes=64)
            for j in range(4):
                src = wraw[s, j, g].bitcast(FP8)
                if (n, j) in V_WIDEN:
                    nc.vector.tensor_scalar(out=t[:, j, :], in0=src, scalar1=scale[:, s, j : j + 1], scalar2=None, op0=MULT)
                else:
                    nc.scalar.activation(t[:, j, :], src, ACT.Copy, scale=scale[:, s, j : j + 1])
            wd[n] = t

        def interleave_wq(n):
            t = new_grp()
            nc.vector.tensor_copy(out=t[:].rearrange("p (t m j) -> p m j t", t=4, j=4), in_=wd[n][:].rearrange("p j (m t) -> p m j t", t=4))
            grp[n] = t

        def interleave_wo(w):
            c, s = divmod(w, 4)
            c0, width = CHUNKS[c]
            t = new_grp()
            src = woraw[c0 // 1024, s][:, :, c0 % 1024 : c0 % 1024 + width]
            o = t[:, : 4 * width].rearrange("p (c i t) -> p c t i", i=4, t=4)
            i = src.rearrange("p t (c i) -> p c t i", i=4)
            if w in S_WO:
                nc.scalar.copy(o, i)
            else:
                nc.vector.tensor_copy(out=o, in_=i)
            grp["o", w] = t

        xq = {}

        xcodes = [stage.tile([P, W], U32, name=f"xq{s}", bufs=1, align_bytes=64) for s in range(4)]
        xscales = [stage.tile([P, W], U8, name=f"xqs{s}", bufs=1, align_bytes=64) for s in range(4)]
        xgrp = {}

        def x_bank(b, s):
            xgrp[b, s] = stage.tile([P, 2 * W], BF16, name="xgrp", bufs=4, align_bytes=64)
            bank = transposed(xraw, s, b, f"b{s}", False)
            dst = xgrp[b, s][:].bitcast(F32).rearrange("p (r u) -> p r u", u=2)
            src = bank[:].rearrange("p (u r) -> p r u", u=2)
            if (b, s) in X_S:
                nc.scalar.copy(dst, src)
            else:
                nc.vector.tensor_copy(out=dst, in_=src)

        def x_quantize(b, s):
            nc.vector.quantize_mx(
                out=xcodes[s][:, b * 256 : (b + 1) * 256].bitcast(FP8X4), scales=xscales[s][:, b * 256 : (b + 1) * 256], in_=xgrp[b, s][:]
            )
            if b == 1:
                xq[s] = xcodes[s], xscales[s]

        abank = {}
        gq = {}
        sig = {}
        acc1 = {}

        def mx1(g, s):
            if s == 0:
                for b in range(2):
                    abank[g, b] = transposed(araw, g, b, f"b{2 * (g % 2) + b}", True)
                for t in range(4):
                    acc1[g, t] = psum.tile([P, T], F32, name=f"a{t}")
            codes, scales = wq[g, s]
            for t in range(4):
                nc.tensor.matmul_mx(
                    out=acc1[g, t][:],
                    lhsT=codes[:, t * P : (t + 1) * P].bitcast(FP8X4),
                    lhsT_scale=scales[:, t * P : (t + 1) * P],
                    rhs=xq[s][0][:].bitcast(FP8X4),
                    rhs_scale=xq[s][1][:],
                    start=(s == 0),
                    stop=(s == 3),
                )

        def sigmoid(g):
            t = stage.tile([P, 4, T], F32, name="sig", bufs=2)
            for k in range(4):
                nc.scalar.activation(t[:, k, :], acc1[g, k][:], ACT.Sigmoid)
            sig[g] = t

        def product(g):
            t = new_grp()
            for b in range(2):
                nc.vector.tensor_tensor(
                    out=t[:, b * 1024 : (b + 1) * 1024].rearrange("p (r i t) -> p r t i", i=4, t=4),
                    in0=abank[g, b][:].bitcast(BF16).rearrange("p (r i t) -> p r t i", i=4, t=4),
                    in1=sig[g][:, :, b * 256 : (b + 1) * 256].rearrange("p t (r i) -> p r t i", i=4),
                    op=MULT,
                )
            grp["g", g] = t

        acc2 = {}

        def mx2(w):
            c, s = divmod(w, 4)
            width = CHUNKS[c][1]
            for i in range(4):
                if s == 0:
                    acc2[c, i] = psum.tile([P, W], F32, name=f"{'ab'[c % 2]}{i}")
                codes, scales = grp["wo", w]
                nc.tensor.matmul_mx(
                    out=acc2[c, i][:, :width],
                    lhsT=gq[s][0][:, i * P : (i + 1) * P].bitcast(FP8X4),
                    lhsT_scale=gq[s][1][:, i * P : (i + 1) * P],
                    rhs=codes[:, :width].bitcast(FP8X4),
                    rhs_scale=scales[:, :width],
                    start=(s == 0),
                    stop=(s == 3),
                )

        def finish(c):
            c0, width = CHUNKS[c]
            for i in range(4):
                o = stage.tile([P, W], F32, name="ost", bufs=OSTB)
                if (c, i) in V_FIN:
                    nc.vector.tensor_copy(out=o[:, :width], in_=acc2[c, i][:, :width])
                else:
                    nc.scalar.copy(o[:, :width], acc2[c, i][:, :width])
                nc.sync.dma_start(out=out_hbm[i * P : (i + 1) * P, c0 : c0 + width], in_=o[:, :width])

        n_wo = 4 * len(CHUNKS)
        events = {}
        pending = {g: [] for g in range(4)}
        open_group = 0
        flushed = {g: 0 for g in range(4)}

        def at(n, f, *a):
            events.setdefault(n, []).append((f, a))

        def put_gq(g):
            gq[g] = quantize(grp["g", g], f"gq{g}", 1, W)

        next_mx2 = 0
        ready_at = {}
        n = 0
        while n < 60:
            if n < 16:
                widen(n)
            for b, s in X_STEPS.get(n, []):
                x_bank(b, s)
            if 0 <= n - LAG < 16:
                interleave_wq(n - LAG)
            for w in range(n_wo):
                if WO0 + w - (S_LEAD if w in S_WO else 0) == n:
                    interleave_wo(w)
            if 0 <= n - QLAG < 16:
                wq[UNITS[n - QLAG]] = quantize(grp[n - QLAG], "wqc", 10, W)
                pending[UNITS[n - QLAG][0]].append(UNITS[n - QLAG][1])
            for b, s in X_STEPS.get(n - 1, []):
                x_quantize(b, s)
            if open_group < 4:
                while flushed[open_group] < len(pending[open_group]) and flushed[open_group] in xq:
                    mx1(open_group, flushed[open_group])
                    flushed[open_group] += 1
                if flushed[open_group] == 4:
                    at(n + SIG_D, sigmoid, open_group)
                    at(n + PROD_D, product, open_group)
                    at(n + GQ_D, put_gq, open_group)
                    flushed[open_group] = 5
            for f, a in events.get(n, []):
                f(*a)
                if f is sigmoid:
                    open_group += 1
            w = n - WO0 - 1
            if 0 <= w < n_wo:
                grp["wo", w] = quantize(grp["o", w], "woc", 8, CHUNKS[w // 4][1])
                ready_at[w] = n + MX2_D - 1
            while next_mx2 in ready_at and ready_at[next_mx2] <= n and (next_mx2 % 4) in gq:
                mx2(next_mx2)
                if next_mx2 % 4 == 3:
                    finish(next_mx2 // 4)
                next_mx2 += 1
            n += 1
